import numpy as np
import ml_dtypes


def mxq(x, axis, fmt="e4m3"):
    dtype, down = {"e4m3": (ml_dtypes.float8_e4m3fn, 7), "e5m2": (ml_dtypes.float8_e5m2, 14)}[fmt]
    v = np.moveaxis(np.asarray(x, np.float32).astype(ml_dtypes.bfloat16).astype(np.float64), axis, -1)
    blocks = v.reshape(v.shape[:-1] + (-1, 32))
    amax = np.abs(blocks).max(-1, keepdims=True)
    byte = np.maximum(np.where(amax > 0, np.frexp(amax)[1] - 1 + 127, 0) - down, 1)
    scale = np.exp2(byte - 127.0)
    codes = (blocks / scale).astype(np.float32).astype(dtype).astype(np.float64)
    return np.moveaxis((codes * scale).reshape(v.shape), -1, axis)


WIDE = False


def mx_kscale(k):
    if not WIDE:
        return np.ones(k)
    levels = np.array([10, -10, 5, -5, 0])
    if k % 512:
        return np.exp2(np.random.permutation(np.resize(levels, k // 32))).repeat(32)
    a = np.empty((k // 512, 16))
    for p in range(k // 512):
        a[p, :8] = np.random.permutation(np.resize(levels, 8))
        for g in range(8):
            far = levels[np.abs(levels - a[p, g]) >= 10]
            a[p, g + 8] = far[np.random.randint(len(far))]
    return np.exp2(a.ravel()).repeat(32)


BF16 = ml_dtypes.bfloat16


def bf(x):
    return np.asarray(x, np.float32).astype(BF16)


def f64(x):
    return np.asarray(x).astype(np.float64)


B, T, C, NH, NKV, HD, P = 8, 1024, 1024, 2, 2, 64, 512


def rope(u, angles):
    up = u.reshape(u.shape[:-1] + (HD // 2, 2))
    cos = np.cos(angles)[None, :, None, :]
    sin = np.sin(angles)[None, :, None, :]
    u0, u1 = up[..., 0], up[..., 1]
    return np.stack([cos * u0 - sin * u1, sin * u0 + cos * u1], axis=-1).reshape(u.shape)


def setup_inputs():
    s = mx_kscale(C)
    return {"x": bf(np.random.standard_normal((B, T, C)) * s),
            "angles": bf(np.random.uniform(-np.pi, np.pi, (T, HD // 2))),
            "wq": bf(np.random.standard_normal((C, NH * HD)) * 0.5 / np.sqrt(C) / s[:, None]),
            "wk": bf(np.random.standard_normal((C, NKV * HD)) * 0.5 / np.sqrt(C) / s[:, None]),
            "wv": bf(np.random.standard_normal((C, NKV * HD)) / np.sqrt(C) / s[:, None])}


def reference(x, angles, wq, wk, wv):
    xq = mxq(f64(x), 2, "e4m3")
    a = f64(angles)
    q = (xq @ mxq(f64(wq), 0, "e4m3")).reshape(B, T, NH, HD)
    k = (xq @ mxq(f64(wk), 0, "e4m3")).reshape(B, T, NKV, HD)
    v = (xq @ mxq(f64(wv), 0, "e4m3")).reshape(B, T, NKV, HD)
    q = rope(q, a)
    k = rope(k, a)
    return q.transpose(0, 2, 1, 3), k.transpose(0, 2, 1, 3), v.transpose(0, 2, 1, 3)

@@ -1,0 +1,210 @@
+import math
+from contextlib import ExitStack
+
+import concourse.mybir as mybir
+from concourse.masks import make_identity
+
+F32 = mybir.dt.float32
+BF16 = mybir.dt.bfloat16
+U32 = mybir.dt.uint32
+U8 = mybir.dt.uint8
+FP8X4 = mybir.dt.float8_e4m3fn_x4
+ALU = mybir.AluOpType
+ACT = mybir.ActivationFunctionType
+
+P = 128
+BATCH, SEQ, C = 8, 1024, 1024
+HEADS, HEAD_DIM = 2, 64
+FEATURES = HEADS * HEAD_DIM
+PAIRS = HEAD_DIM // 2
+PACK = 4
+K_PASS = P * PACK
+PASSES = C // K_PASS
+WORDS = C // 2
+TILES = SEQ // P
+LOAD_TILES = 4
+DUO = 2
+LOADS = BATCH * TILES // LOAD_TILES
+DUOS = BATCH * TILES // DUO
+DUOS_PER_BATCH = TILES // DUO
+DUOS_PER_LOAD = LOAD_TILES // DUO
+ROTATED_HEADS = 2 * HEADS
+LOADS_AHEAD = 8
+
+FLOPS = 2 * BATCH * SEQ * C * 3 * FEATURES
+
+
+def tile_groupqueryatention_pa_t_kernel(tc, x, angles, wq, wk, wv, out_0, out_1, out_2):
+    nc = tc.nc
+    with ExitStack() as ctx:
+        const = ctx.enter_context(tc.tile_pool(name="const", bufs=1))
+        x_pool = ctx.enter_context(tc.tile_pool(name="x", bufs=LOADS_AHEAD))
+        stage = ctx.enter_context(tc.tile_pool(name="stage", bufs=3))
+        results = ctx.enter_context(tc.tile_pool(name="results", bufs=3))
+        psum_xt = ctx.enter_context(tc.psum_pool(name="psum_xt", bufs=4))
+        psum_qk = ctx.enter_context(tc.psum_pool(name="psum_qk", bufs=2))
+        psum_v = ctx.enter_context(tc.psum_pool(name="psum_v", bufs=2))
+
+        x_tiles = {}
+
+        def load_x(n):
+            b, half = divmod(n, TILES // LOAD_TILES)
+            x_sb = x_pool.tile([P, LOAD_TILES, C], BF16)
+            rows = x[b].rearrange("(p j) c -> p j c", j=TILES)
+            nc.sync.dma_start(out=x_sb[:], in_=rows[:, half * LOAD_TILES : (half + 1) * LOAD_TILES, :])
+            x_tiles[n] = x_sb
+
+        load_x(0)
+        w_raw = const.tile([P, 3, PASSES, PACK, FEATURES], BF16)
+        for m, w in enumerate((wq, wk, wv)):
+            nc.scalar.dma_start(
+                out=w_raw[:, m].rearrange("p g t n -> p g (t n)"),
+                in_=w.rearrange("(g p t) n -> p g (t n)", g=PASSES, t=PACK),
+            )
+        angles_bf = const.tile([P, TILES, PAIRS], BF16)
+        nc.scalar.dma_start(out=angles_bf[:], in_=angles.rearrange("(p j) i -> p j i", j=TILES))
+        for n in range(1, LOADS_AHEAD):
+            load_x(n)
+
+        identity = const.tile([P, P], F32)
+        make_identity(nc, identity[:])
+
+        wqk_grouped = const.tile([P, PASSES, 2 * FEATURES, PACK], BF16, align_bytes=64)
+        wv_grouped = const.tile([P, PASSES, FEATURES, PACK], BF16, align_bytes=64)
+        for g in range(PASSES):
+            nc.vector.tensor_copy(
+                out=wqk_grouped[:, g].rearrange("p (m n) t -> p m n t", m=2),
+                in_=w_raw[:, 0:2, g].rearrange("p m t n -> p m n t"),
+            )
+            nc.vector.tensor_copy(out=wv_grouped[:, g], in_=w_raw[:, 2, g].rearrange("p t n -> p n t"))
+        wqk_codes = const.tile([P, PASSES, 2 * FEATURES], U32, align_bytes=64)
+        wqk_scales = const.tile([P, PASSES, 2 * FEATURES], U8, align_bytes=64)
+        wv_codes = const.tile([P, PASSES, FEATURES], U32, align_bytes=64)
+        wv_scales = const.tile([P, PASSES, FEATURES], U8, align_bytes=64)
+        nc.vector.quantize_mx(
+            out=wqk_codes[:].rearrange("p g n -> p (g n)").bitcast(FP8X4),
+            scales=wqk_scales[:].rearrange("p g n -> p (g n)"),
+            in_=wqk_grouped[:].rearrange("p g n t -> p (g n t)"),
+        )
+        nc.vector.quantize_mx(
+            out=wv_codes[:].rearrange("p g n -> p (g n)").bitcast(FP8X4),
+            scales=wv_scales[:].rearrange("p g n -> p (g n)"),
+            in_=wv_grouped[:].rearrange("p g n t -> p (g n t)"),
+        )
+
+        angle = const.tile([P, TILES, PAIRS], F32)
+        nc.vector.tensor_copy(out=angle[:], in_=angles_bf[:])
+        abs_angle = const.tile([P, TILES, PAIRS], F32)
+        nc.vector.scalar_tensor_tensor(
+            out=abs_angle[:], in0=angle[:], scalar=-1.0, in1=angle[:], op0=ALU.mult, op1=ALU.max
+        )
+        cos_arg = const.tile([P, TILES, PAIRS], F32)
+        nc.vector.tensor_scalar(
+            out=cos_arg[:], in0=abs_angle[:], scalar1=-1.0, scalar2=math.pi / 2, op0=ALU.mult, op1=ALU.add
+        )
+        cos_sin = const.tile([P, TILES, PAIRS, 2], F32)
+        negsin_cos = const.tile([P, TILES, PAIRS, 2], F32)
+        nc.scalar.activation(out=cos_sin[:, :, :, 0], in_=cos_arg[:], func=ACT.Sin)
+        nc.scalar.activation(out=cos_sin[:, :, :, 1], in_=angle[:], func=ACT.Sin)
+        nc.scalar.activation(out=negsin_cos[:, :, :, 0], in_=angle[:], func=ACT.Sin, scale=-1.0)
+        nc.scalar.activation(out=negsin_cos[:, :, :, 1], in_=cos_arg[:], func=ACT.Sin)
+
+        grouped_tiles = {}
+        x_operands = {}
+        sums = {}
+        batch_tiles = {}
+
+        def transpose_duo(d):
+            x_words = x_tiles[d // DUOS_PER_LOAD][:].bitcast(F32)
+            grouped = stage.tile([P, DUO, PASSES, P, 2], F32, align_bytes=64)
+            for a in range(DUO):
+                j = (d % DUOS_PER_LOAD) * DUO + a
+                xt = psum_xt.tile([P, WORDS // P, P], F32)
+                for c in range(WORDS // P):
+                    g, u = divmod(c, 2)
+                    words = x_words[:, j, g * 2 * P + u : (g + 1) * 2 * P : 2]
+                    nc.tensor.transpose(xt[:, c, :], words, identity[:])
+                nc.scalar.copy(out=grouped[:, a], in_=xt[:].rearrange("p (g u) r -> p g r u", u=2))
+            grouped_tiles[d] = grouped
+
+        def quantise_duo(d):
+            codes = stage.tile([P, DUO, PASSES, P], U32, align_bytes=64)
+            scales = stage.tile([P, DUO, PASSES, P], U8, align_bytes=64)
+            nc.vector.quantize_mx(
+                out=codes[:].rearrange("p a g r -> p (a g r)").bitcast(FP8X4),
+                scales=scales[:].rearrange("p a g r -> p (a g r)"),
+                in_=grouped_tiles[d][:].rearrange("p a g r u -> p (a g r u)").bitcast(BF16),
+            )
+            x_operands[d] = (codes, scales)
+
+        def project_duo(d):
+            codes, scales = x_operands[d]
+            qk_ps = psum_qk.tile([P, DUO, 2 * FEATURES], F32)
+            v_ps = psum_v.tile([P, DUO, FEATURES], F32)
+            for a in range(DUO):
+                for acc, w_codes, w_scales in ((qk_ps, wqk_codes, wqk_scales), (v_ps, wv_codes, wv_scales)):
+                    for g in range(PASSES):
+                        nc.tensor.matmul_mx(
+                            out=acc[:, a, :],
+                            lhsT=codes[:, a, g, :].bitcast(FP8X4),
+                            lhsT_scale=scales[:, a, g, :],
+                            rhs=w_codes[:, g, :].bitcast(FP8X4),
+                            rhs_scale=w_scales[:, g, :],
+                            start=(g == 0),
+                            stop=(g == PASSES - 1),
+                        )
+            sums[d] = (qk_ps, v_ps)
+
+        def rotate_duo(d):
+            b, part = divmod(d, DUOS_PER_BATCH)
+            if part == 0:
+                rotated = results.tile([P, ROTATED_HEADS, TILES, HEAD_DIM], F32)
+                odd_part = results.tile([P, ROTATED_HEADS, TILES, HEAD_DIM], F32)
+                v_sb = results.tile([P, HEADS, TILES, HEAD_DIM], F32)
+                batch_tiles[b] = (rotated, odd_part, v_sb)
+            rotated, odd_part, v_sb = batch_tiles[b]
+            qk_ps, v_ps = sums[d]
+            js = slice(part * DUO, (part + 1) * DUO)
+            shape = [P, DUO, ROTATED_HEADS, PAIRS, 2]
+            pairs = qk_ps[:].rearrange("p a (q i two) -> p a q i two", q=ROTATED_HEADS, two=2)
+            nc.vector.tensor_tensor(
+                out=rotated[:, :, js, :].rearrange("p q a (i two) -> p a q i two", two=2),
+                in0=pairs[:, :, :, :, 0:1].to_broadcast(shape),
+                in1=cos_sin[:, js].unsqueeze(2).to_broadcast(shape),
+                op=ALU.mult,
+            )
+            nc.vector.tensor_tensor(
+                out=odd_part[:, :, js, :].rearrange("p q a (i two) -> p a q i two", two=2),
+                in0=pairs[:, :, :, :, 1:2].to_broadcast(shape),
+                in1=negsin_cos[:, js].unsqueeze(2).to_broadcast(shape),
+                op=ALU.mult,
+            )
+            nc.scalar.copy(
+                out=v_sb[:, :, js, :].rearrange("p h a d -> p a h d"),
+                in_=v_ps[:].rearrange("p a (h d) -> p a h d", h=HEADS),
+            )
+            nc.vector.tensor_tensor(
+                out=rotated[:, :, js, :], in0=rotated[:, :, js, :], in1=odd_part[:, :, js, :], op=ALU.add
+            )
+
+        def store_batch(b):
+            rotated, odd_part, v_sb = batch_tiles[b]
+            for dram, heads in ((out_0, rotated[:, 0:HEADS]), (out_1, rotated[:, HEADS:]), (out_2, v_sb[:])):
+                nc.sync.dma_start(
+                    out=dram[b].rearrange("h (p j) d -> p h (j d)", j=TILES),
+                    in_=heads.rearrange("p h j d -> p h (j d)"),
+                )
+
+        transpose_duo(0)
+        quantise_duo(0)
+        for d in range(DUOS):
+            if d + 1 < DUOS:
+                transpose_duo(d + 1)
+            project_duo(d)
+            if d + 1 < DUOS:
+                quantise_duo(d + 1)
+            rotate_duo(d)
+            if d % DUOS_PER_LOAD == DUOS_PER_LOAD - 1 and d // DUOS_PER_LOAD + LOADS_AHEAD < LOADS:
+                load_x(d // DUOS_PER_LOAD + LOADS_AHEAD)
+            if d % DUOS_PER_BATCH == DUOS_PER_BATCH - 1:
+                store_batch(d // DUOS_PER_BATCH)

@@ -22,14 +22,13 @@ K_PASS = P * PACK
 PASSES = C // K_PASS
 WORDS = C // 2
 TILES = SEQ // P
-LOAD_TILES = 4
+QUAD = 4
 DUO = 2
-LOADS = BATCH * TILES // LOAD_TILES
-DUOS = BATCH * TILES // DUO
-DUOS_PER_BATCH = TILES // DUO
-DUOS_PER_LOAD = LOAD_TILES // DUO
+QUADS = BATCH * TILES // QUAD
+QUADS_PER_BATCH = TILES // QUAD
+DUOS = QUAD // DUO
 ROTATED_HEADS = 2 * HEADS
-LOADS_AHEAD = 8
+LOADS_AHEAD = 12
 
 FLOPS = 2 * BATCH * SEQ * C * 3 * FEATURES
 
@@ -42,32 +41,49 @@ def tile_groupqueryatention_pa_t_kernel(tc, x, angles, wq, wk, wv, out_0, out_1,
         stage = ctx.enter_context(tc.tile_pool(name="stage", bufs=3))
         results = ctx.enter_context(tc.tile_pool(name="results", bufs=3))
         psum_xt = ctx.enter_context(tc.psum_pool(name="psum_xt", bufs=4))
-        psum_qk = ctx.enter_context(tc.psum_pool(name="psum_qk", bufs=2))
-        psum_v = ctx.enter_context(tc.psum_pool(name="psum_v", bufs=2))
+        psum_qk = ctx.enter_context(tc.psum_pool(name="psum_qk", bufs=3))
+        psum_v = ctx.enter_context(tc.psum_pool(name="psum_v", bufs=1))
+        ctx.enter_context(tc.manual_schedule())
 
         x_tiles = {}
 
-        def load_x(n):
-            b, half = divmod(n, TILES // LOAD_TILES)
-            x_sb = x_pool.tile([P, LOAD_TILES, C], BF16)
+        def load_x(n, pieces=1):
+            b, half = divmod(n, QUADS_PER_BATCH)
+            x_sb = x_pool.tile([P, QUAD, C], BF16)
             rows = x[b].rearrange("(p j) c -> p j c", j=TILES)
-            nc.sync.dma_start(out=x_sb[:], in_=rows[:, half * LOAD_TILES : (half + 1) * LOAD_TILES, :])
+            step = QUAD // pieces
+            for i in range(0, QUAD, step):
+                nc.sync.dma_start(
+                    out=x_sb[:, i : i + step, :], in_=rows[:, half * QUAD + i : half * QUAD + i + step, :]
+                )
             x_tiles[n] = x_sb
 
-        load_x(0)
+        load_x(0, pieces=QUAD)
+        angles_bf = const.tile([P, TILES, PAIRS], BF16)
+        nc.scalar.dma_start(out=angles_bf[:], in_=angles.rearrange("(p j) i -> p j i", j=TILES))
         w_raw = const.tile([P, 3, PASSES, PACK, FEATURES], BF16)
         for m, w in enumerate((wq, wk, wv)):
             nc.scalar.dma_start(
                 out=w_raw[:, m].rearrange("p g t n -> p g (t n)"),
                 in_=w.rearrange("(g p t) n -> p g (t n)", g=PASSES, t=PACK),
             )
-        angles_bf = const.tile([P, TILES, PAIRS], BF16)
-        nc.scalar.dma_start(out=angles_bf[:], in_=angles.rearrange("(p j) i -> p j i", j=TILES))
         for n in range(1, LOADS_AHEAD):
             load_x(n)
 
         identity = const.tile([P, P], F32)
         make_identity(nc, identity[:])
+
+        cos_arg = const.tile([P, TILES, PAIRS], F32)
+        nc.vector.scalar_tensor_tensor(
+            out=cos_arg[:], in0=angles_bf[:], scalar=-1.0, in1=angles_bf[:], op0=ALU.mult, op1=ALU.max
+        )
+        nc.vector.tensor_scalar(
+            out=cos_arg[:], in0=cos_arg[:], scalar1=-1.0, scalar2=math.pi / 2, op0=ALU.mult, op1=ALU.add
+        )
+        trig = const.tile([P, TILES, 3, PAIRS], F32)
+        nc.scalar.activation(out=trig[:, :, 2, :], in_=angles_bf[:], func=ACT.Sin)
+        nc.scalar.activation(out=trig[:, :, 0, :], in_=angles_bf[:], func=ACT.Sin, scale=-1.0)
+        nc.scalar.activation(out=trig[:, :, 1, :], in_=cos_arg[:], func=ACT.Sin)
 
         wqk_grouped = const.tile([P, PASSES, 2 * FEATURES, PACK], BF16, align_bytes=64)
         wv_grouped = const.tile([P, PASSES, FEATURES, PACK], BF16, align_bytes=64)
@@ -76,6 +92,7 @@ def tile_groupqueryatention_pa_t_kernel(tc, x, angles, wq, wk, wv, out_0, out_1,
                 out=wqk_grouped[:, g].rearrange("p (m n) t -> p m n t", m=2),
                 in_=w_raw[:, 0:2, g].rearrange("p m t n -> p m n t"),
             )
+        for g in range(PASSES):
             nc.vector.tensor_copy(out=wv_grouped[:, g], in_=w_raw[:, 2, g].rearrange("p t n -> p n t"))
         wqk_codes = const.tile([P, PASSES, 2 * FEATURES], U32, align_bytes=64)
         wqk_scales = const.tile([P, PASSES, 2 * FEATURES], U8, align_bytes=64)
@@ -92,60 +109,55 @@ def tile_groupqueryatention_pa_t_kernel(tc, x, angles, wq, wk, wv, out_0, out_1,
             in_=wv_grouped[:].rearrange("p g n t -> p (g n t)"),
         )
 
-        angle = const.tile([P, TILES, PAIRS], F32)
-        nc.vector.tensor_copy(out=angle[:], in_=angles_bf[:])
-        abs_angle = const.tile([P, TILES, PAIRS], F32)
-        nc.vector.scalar_tensor_tensor(
-            out=abs_angle[:], in0=angle[:], scalar=-1.0, in1=angle[:], op0=ALU.mult, op1=ALU.max
-        )
-        cos_arg = const.tile([P, TILES, PAIRS], F32)
-        nc.vector.tensor_scalar(
-            out=cos_arg[:], in0=abs_angle[:], scalar1=-1.0, scalar2=math.pi / 2, op0=ALU.mult, op1=ALU.add
-        )
         cos_sin = const.tile([P, TILES, PAIRS, 2], F32)
         negsin_cos = const.tile([P, TILES, PAIRS, 2], F32)
-        nc.scalar.activation(out=cos_sin[:, :, :, 0], in_=cos_arg[:], func=ACT.Sin)
-        nc.scalar.activation(out=cos_sin[:, :, :, 1], in_=angle[:], func=ACT.Sin)
-        nc.scalar.activation(out=negsin_cos[:, :, :, 0], in_=angle[:], func=ACT.Sin, scale=-1.0)
-        nc.scalar.activation(out=negsin_cos[:, :, :, 1], in_=cos_arg[:], func=ACT.Sin)
+
+        def interleave_tables():
+            nc.vector.tensor_copy(out=cos_sin[:], in_=trig[:, :, 1:3].rearrange("p j two i -> p j i two"))
+            nc.vector.tensor_copy(out=negsin_cos[:], in_=trig[:, :, 0:2].rearrange("p j two i -> p j i two"))
 
         grouped_tiles = {}
         x_operands = {}
         sums = {}
         batch_tiles = {}
 
-        def transpose_duo(d):
-            x_words = x_tiles[d // DUOS_PER_LOAD][:].bitcast(F32)
-            grouped = stage.tile([P, DUO, PASSES, P, 2], F32, align_bytes=64)
-            for a in range(DUO):
-                j = (d % DUOS_PER_LOAD) * DUO + a
+        def transpose_quad(n):
+            x_words = x_tiles[n][:].bitcast(F32)
+            grouped = stage.tile([P, QUAD, PASSES, P, 2], F32, align_bytes=64)
+            for a in range(QUAD):
                 xt = psum_xt.tile([P, WORDS // P, P], F32)
                 for c in range(WORDS // P):
                     g, u = divmod(c, 2)
-                    words = x_words[:, j, g * 2 * P + u : (g + 1) * 2 * P : 2]
+                    words = x_words[:, a, g * 2 * P + u : (g + 1) * 2 * P : 2]
                     nc.tensor.transpose(xt[:, c, :], words, identity[:])
                 nc.scalar.copy(out=grouped[:, a], in_=xt[:].rearrange("p (g u) r -> p g r u", u=2))
-            grouped_tiles[d] = grouped
+            grouped_tiles[n] = grouped
 
-        def quantise_duo(d):
-            codes = stage.tile([P, DUO, PASSES, P], U32, align_bytes=64)
-            scales = stage.tile([P, DUO, PASSES, P], U8, align_bytes=64)
+        def quantise_quad(n):
+            codes = stage.tile([P, QUAD, PASSES, P], U32, align_bytes=64)
+            scales = stage.tile([P, QUAD, PASSES, P], U8, align_bytes=64)
             nc.vector.quantize_mx(
                 out=codes[:].rearrange("p a g r -> p (a g r)").bitcast(FP8X4),
                 scales=scales[:].rearrange("p a g r -> p (a g r)"),
-                in_=grouped_tiles[d][:].rearrange("p a g r u -> p (a g r u)").bitcast(BF16),
+                in_=grouped_tiles[n][:].rearrange("p a g r u -> p (a g r u)").bitcast(BF16),
             )
-            x_operands[d] = (codes, scales)
+            x_operands[n] = (codes, scales)
 
-        def project_duo(d):
-            codes, scales = x_operands[d]
-            qk_ps = psum_qk.tile([P, DUO, 2 * FEATURES], F32)
-            v_ps = psum_v.tile([P, DUO, FEATURES], F32)
-            for a in range(DUO):
-                for acc, w_codes, w_scales in ((qk_ps, wqk_codes, wqk_scales), (v_ps, wv_codes, wv_scales)):
+        def project_quad(n):
+            codes, scales = x_operands[n]
+            v_ps = psum_v.tile([P, QUAD, FEATURES], F32)
+            qk_banks = []
+            for a in range(QUAD):
+                if a % DUO == 0:
+                    qk_ps = psum_qk.tile([P, DUO, 2 * FEATURES], F32)
+                    qk_banks.append(qk_ps)
+                for acc, w_codes, w_scales in (
+                    (qk_ps[:, a % DUO, :], wqk_codes, wqk_scales),
+                    (v_ps[:, a, :], wv_codes, wv_scales),
+                ):
                     for g in range(PASSES):
                         nc.tensor.matmul_mx(
-                            out=acc[:, a, :],
+                            out=acc,
                             lhsT=codes[:, a, g, :].bitcast(FP8X4),
                             lhsT_scale=scales[:, a, g, :],
                             rhs=w_codes[:, g, :].bitcast(FP8X4),
@@ -153,18 +165,20 @@ def tile_groupqueryatention_pa_t_kernel(tc, x, angles, wq, wk, wv, out_0, out_1,
                             start=(g == 0),
                             stop=(g == PASSES - 1),
                         )
-            sums[d] = (qk_ps, v_ps)
+            sums[n] = (qk_banks, v_ps)
 
-        def rotate_duo(d):
-            b, part = divmod(d, DUOS_PER_BATCH)
-            if part == 0:
-                rotated = results.tile([P, ROTATED_HEADS, TILES, HEAD_DIM], F32)
-                odd_part = results.tile([P, ROTATED_HEADS, TILES, HEAD_DIM], F32)
-                v_sb = results.tile([P, HEADS, TILES, HEAD_DIM], F32)
-                batch_tiles[b] = (rotated, odd_part, v_sb)
-            rotated, odd_part, v_sb = batch_tiles[b]
-            qk_ps, v_ps = sums[d]
-            js = slice(part * DUO, (part + 1) * DUO)
+        def open_batch(b):
+            rotated = results.tile([P, ROTATED_HEADS, TILES, HEAD_DIM], F32)
+            v_sb = results.tile([P, HEADS, TILES, HEAD_DIM], F32)
+            batch_tiles[b] = (rotated, v_sb)
+
+        def rotate_duo(n, i, adder):
+            b, half = divmod(n, QUADS_PER_BATCH)
+            rotated = batch_tiles[b][0]
+            qk_ps = sums[n][0][i]
+            j0 = half * QUAD + i * DUO
+            js = slice(j0, j0 + DUO)
+            odd_part = results.tile([P, ROTATED_HEADS, DUO, HEAD_DIM], F32)
             shape = [P, DUO, ROTATED_HEADS, PAIRS, 2]
             pairs = qk_ps[:].rearrange("p a (q i two) -> p a q i two", q=ROTATED_HEADS, two=2)
             nc.vector.tensor_tensor(
@@ -174,37 +188,45 @@ def tile_groupqueryatention_pa_t_kernel(tc, x, angles, wq, wk, wv, out_0, out_1,
                 op=ALU.mult,
             )
             nc.vector.tensor_tensor(
-                out=odd_part[:, :, js, :].rearrange("p q a (i two) -> p a q i two", two=2),
+                out=odd_part[:].rearrange("p q a (i two) -> p a q i two", two=2),
                 in0=pairs[:, :, :, :, 1:2].to_broadcast(shape),
                 in1=negsin_cos[:, js].unsqueeze(2).to_broadcast(shape),
                 op=ALU.mult,
             )
+            adder.tensor_tensor(out=rotated[:, :, js, :], in0=rotated[:, :, js, :], in1=odd_part[:], op=ALU.add)
+
+        def copy_v(n):
+            b, half = divmod(n, QUADS_PER_BATCH)
+            js = slice(half * QUAD, (half + 1) * QUAD)
             nc.scalar.copy(
-                out=v_sb[:, :, js, :].rearrange("p h a d -> p a h d"),
-                in_=v_ps[:].rearrange("p a (h d) -> p a h d", h=HEADS),
-            )
-            nc.vector.tensor_tensor(
-                out=rotated[:, :, js, :], in0=rotated[:, :, js, :], in1=odd_part[:, :, js, :], op=ALU.add
+                out=batch_tiles[b][1][:, :, js, :].rearrange("p h a d -> p a h d"),
+                in_=sums[n][1][:].rearrange("p a (h d) -> p a h d", h=HEADS),
             )
 
         def store_batch(b):
-            rotated, odd_part, v_sb = batch_tiles[b]
+            rotated, v_sb = batch_tiles[b]
             for dram, heads in ((out_0, rotated[:, 0:HEADS]), (out_1, rotated[:, HEADS:]), (out_2, v_sb[:])):
                 nc.sync.dma_start(
                     out=dram[b].rearrange("h (p j) d -> p h (j d)", j=TILES),
                     in_=heads.rearrange("p h j d -> p h (j d)"),
                 )
 
-        transpose_duo(0)
-        quantise_duo(0)
-        for d in range(DUOS):
-            if d + 1 < DUOS:
-                transpose_duo(d + 1)
-            project_duo(d)
-            if d + 1 < DUOS:
-                quantise_duo(d + 1)
-            rotate_duo(d)
-            if d % DUOS_PER_LOAD == DUOS_PER_LOAD - 1 and d // DUOS_PER_LOAD + LOADS_AHEAD < LOADS:
-                load_x(d // DUOS_PER_LOAD + LOADS_AHEAD)
-            if d % DUOS_PER_BATCH == DUOS_PER_BATCH - 1:
-                store_batch(d // DUOS_PER_BATCH)
+        transpose_quad(0)
+        quantise_quad(0)
+        interleave_tables()
+        for n in range(QUADS):
+            last = n + 1 == QUADS
+            if n % QUADS_PER_BATCH == 0:
+                open_batch(n // QUADS_PER_BATCH)
+            if not last:
+                transpose_quad(n + 1)
+            project_quad(n)
+            rotate_duo(n, 0, nc.gpsimd)
+            if not last:
+                quantise_quad(n + 1)
+            rotate_duo(n, 1, nc.vector if last else nc.gpsimd)
+            copy_v(n)
+            if n + LOADS_AHEAD < QUADS:
+                load_x(n + LOADS_AHEAD)
+            if n % QUADS_PER_BATCH == QUADS_PER_BATCH - 1:
+                store_batch(n // QUADS_PER_BATCH)

@@ -26,7 +26,9 @@ QUAD = 4
 DUO = 2
 QUADS = BATCH * TILES // QUAD
 QUADS_PER_BATCH = TILES // QUAD
-DUOS = QUAD // DUO
+DUOS = BATCH * TILES // DUO
+DUOS_PER_QUAD = QUAD // DUO
+DUOS_PER_BATCH = TILES // DUO
 ROTATED_HEADS = 2 * HEADS
 LOADS_AHEAD = 12
 
@@ -121,43 +123,38 @@ def tile_groupqueryatention_pa_t_kernel(tc, x, angles, wq, wk, wv, out_0, out_1,
         sums = {}
         batch_tiles = {}
 
-        def transpose_quad(n):
-            x_words = x_tiles[n][:].bitcast(F32)
-            grouped = stage.tile([P, QUAD, PASSES, P, 2], F32, align_bytes=64)
-            for a in range(QUAD):
+        def transpose_duo(d):
+            x_words = x_tiles[d // DUOS_PER_QUAD][:].bitcast(F32)
+            grouped = stage.tile([P, DUO, PASSES, P, 2], F32, align_bytes=64)
+            for a in range(DUO):
+                j = (d % DUOS_PER_QUAD) * DUO + a
                 xt = psum_xt.tile([P, WORDS // P, P], F32)
                 for c in range(WORDS // P):
                     g, u = divmod(c, 2)
-                    words = x_words[:, a, g * 2 * P + u : (g + 1) * 2 * P : 2]
+                    words = x_words[:, j, g * 2 * P + u : (g + 1) * 2 * P : 2]
                     nc.tensor.transpose(xt[:, c, :], words, identity[:])
                 nc.scalar.copy(out=grouped[:, a], in_=xt[:].rearrange("p (g u) r -> p g r u", u=2))
-            grouped_tiles[n] = grouped
+            grouped_tiles[d] = grouped
 
-        def quantise_quad(n):
-            codes = stage.tile([P, QUAD, PASSES, P], U32, align_bytes=64)
-            scales = stage.tile([P, QUAD, PASSES, P], U8, align_bytes=64)
+        def quantise_duo(d):
+            codes = stage.tile([P, DUO, PASSES, P], U32, align_bytes=64)
+            scales = stage.tile([P, DUO, PASSES, P], U8, align_bytes=64)
             nc.vector.quantize_mx(
                 out=codes[:].rearrange("p a g r -> p (a g r)").bitcast(FP8X4),
                 scales=scales[:].rearrange("p a g r -> p (a g r)"),
-                in_=grouped_tiles[n][:].rearrange("p a g r u -> p (a g r u)").bitcast(BF16),
+                in_=grouped_tiles[d][:].rearrange("p a g r u -> p (a g r u)").bitcast(BF16),
             )
-            x_operands[n] = (codes, scales)
+            x_operands[d] = (codes, scales)
 
-        def project_quad(n):
-            codes, scales = x_operands[n]
-            v_ps = psum_v.tile([P, QUAD, FEATURES], F32)
-            qk_banks = []
-            for a in range(QUAD):
-                if a % DUO == 0:
-                    qk_ps = psum_qk.tile([P, DUO, 2 * FEATURES], F32)
-                    qk_banks.append(qk_ps)
-                for acc, w_codes, w_scales in (
-                    (qk_ps[:, a % DUO, :], wqk_codes, wqk_scales),
-                    (v_ps[:, a, :], wv_codes, wv_scales),
-                ):
+        def project_duo(d):
+            codes, scales = x_operands[d]
+            qk_ps = psum_qk.tile([P, DUO, 2 * FEATURES], F32)
+            v_ps = psum_v.tile([P, DUO, FEATURES], F32)
+            for a in range(DUO):
+                for acc, w_codes, w_scales in ((qk_ps, wqk_codes, wqk_scales), (v_ps, wv_codes, wv_scales)):
                     for g in range(PASSES):
                         nc.tensor.matmul_mx(
-                            out=acc,
+                            out=acc[:, a, :],
                             lhsT=codes[:, a, g, :].bitcast(FP8X4),
                             lhsT_scale=scales[:, a, g, :],
                             rhs=w_codes[:, g, :].bitcast(FP8X4),
@@ -165,19 +162,18 @@ def tile_groupqueryatention_pa_t_kernel(tc, x, angles, wq, wk, wv, out_0, out_1,
                             start=(g == 0),
                             stop=(g == PASSES - 1),
                         )
-            sums[n] = (qk_banks, v_ps)
+            sums[d] = (qk_ps, v_ps)
 
         def open_batch(b):
             rotated = results.tile([P, ROTATED_HEADS, TILES, HEAD_DIM], F32)
             v_sb = results.tile([P, HEADS, TILES, HEAD_DIM], F32)
             batch_tiles[b] = (rotated, v_sb)
 
-        def rotate_duo(n, i, adder):
-            b, half = divmod(n, QUADS_PER_BATCH)
+        def rotate_duo(d, adder):
+            b, part = divmod(d, DUOS_PER_BATCH)
             rotated = batch_tiles[b][0]
-            qk_ps = sums[n][0][i]
-            j0 = half * QUAD + i * DUO
-            js = slice(j0, j0 + DUO)
+            qk_ps = sums[d][0]
+            js = slice(part * DUO, (part + 1) * DUO)
             odd_part = results.tile([P, ROTATED_HEADS, DUO, HEAD_DIM], F32)
             shape = [P, DUO, ROTATED_HEADS, PAIRS, 2]
             pairs = qk_ps[:].rearrange("p a (q i two) -> p a q i two", q=ROTATED_HEADS, two=2)
@@ -195,38 +191,42 @@ def tile_groupqueryatention_pa_t_kernel(tc, x, angles, wq, wk, wv, out_0, out_1,
             )
             adder.tensor_tensor(out=rotated[:, :, js, :], in0=rotated[:, :, js, :], in1=odd_part[:], op=ALU.add)
 
-        def copy_v(n):
-            b, half = divmod(n, QUADS_PER_BATCH)
-            js = slice(half * QUAD, (half + 1) * QUAD)
+        def copy_v(d):
+            b, part = divmod(d, DUOS_PER_BATCH)
+            js = slice(part * DUO, (part + 1) * DUO)
             nc.scalar.copy(
                 out=batch_tiles[b][1][:, :, js, :].rearrange("p h a d -> p a h d"),
-                in_=sums[n][1][:].rearrange("p a (h d) -> p a h d", h=HEADS),
+                in_=sums[d][1][:].rearrange("p a (h d) -> p a h d", h=HEADS),
             )
 
-        def store_batch(b):
+        def store(b, j0, j1):
             rotated, v_sb = batch_tiles[b]
-            for dram, heads in ((out_0, rotated[:, 0:HEADS]), (out_1, rotated[:, HEADS:]), (out_2, v_sb[:])):
+            for dram, heads in ((out_2, v_sb[:]), (out_0, rotated[:, 0:HEADS]), (out_1, rotated[:, HEADS:])):
                 nc.sync.dma_start(
-                    out=dram[b].rearrange("h (p j) d -> p h (j d)", j=TILES),
-                    in_=heads.rearrange("p h j d -> p h (j d)"),
+                    out=dram[b].rearrange("h (p j) d -> p h j d", j=TILES)[:, :, j0:j1, :],
+                    in_=heads[:, :, j0:j1, :],
                 )
 
-        transpose_quad(0)
-        quantise_quad(0)
+        transpose_duo(0)
+        quantise_duo(0)
         interleave_tables()
-        for n in range(QUADS):
-            last = n + 1 == QUADS
-            if n % QUADS_PER_BATCH == 0:
-                open_batch(n // QUADS_PER_BATCH)
+        for d in range(DUOS):
+            b, part = divmod(d, DUOS_PER_BATCH)
+            last = d + 1 == DUOS
+            if part == 0:
+                open_batch(b)
             if not last:
-                transpose_quad(n + 1)
-            project_quad(n)
-            rotate_duo(n, 0, nc.gpsimd)
+                transpose_duo(d + 1)
+            project_duo(d)
             if not last:
-                quantise_quad(n + 1)
-            rotate_duo(n, 1, nc.vector if last else nc.gpsimd)
-            copy_v(n)
-            if n + LOADS_AHEAD < QUADS:
-                load_x(n + LOADS_AHEAD)
-            if n % QUADS_PER_BATCH == QUADS_PER_BATCH - 1:
-                store_batch(n // QUADS_PER_BATCH)
+                quantise_duo(d + 1)
+            rotate_duo(d, nc.vector if last else nc.gpsimd)
+            copy_v(d)
+            quad, rest = divmod(d + 1, DUOS_PER_QUAD)
+            if rest == 0 and quad - 1 + LOADS_AHEAD < QUADS:
+                load_x(quad - 1 + LOADS_AHEAD)
+            if b + 1 < BATCH:
+                if part + 1 == DUOS_PER_BATCH:
+                    store(b, 0, TILES)
+            else:
+                store(b, part * DUO, (part + 1) * DUO)

@@ -30,6 +30,7 @@ DUOS = BATCH * TILES // DUO
 DUOS_PER_QUAD = QUAD // DUO
 DUOS_PER_BATCH = TILES // DUO
 ROTATED_HEADS = 2 * HEADS
+AHEAD = 2
 LOADS_AHEAD = 12
 
 FLOPS = 2 * BATCH * SEQ * C * 3 * FEATURES
@@ -40,7 +41,7 @@ def tile_groupqueryatention_pa_t_kernel(tc, x, angles, wq, wk, wv, out_0, out_1,
     with ExitStack() as ctx:
         const = ctx.enter_context(tc.tile_pool(name="const", bufs=1))
         x_pool = ctx.enter_context(tc.tile_pool(name="x", bufs=LOADS_AHEAD))
-        stage = ctx.enter_context(tc.tile_pool(name="stage", bufs=3))
+        stage = ctx.enter_context(tc.tile_pool(name="stage", bufs=AHEAD + 2))
         results = ctx.enter_context(tc.tile_pool(name="results", bufs=3))
         psum_xt = ctx.enter_context(tc.psum_pool(name="psum_xt", bufs=4))
         psum_qk = ctx.enter_context(tc.psum_pool(name="psum_qk", bufs=3))
@@ -207,20 +208,21 @@ def tile_groupqueryatention_pa_t_kernel(tc, x, angles, wq, wk, wv, out_0, out_1,
                     in_=heads[:, :, j0:j1, :],
                 )
 
-        transpose_duo(0)
-        quantise_duo(0)
+        for d in range(AHEAD):
+            transpose_duo(d)
+            quantise_duo(d)
         interleave_tables()
         for d in range(DUOS):
             b, part = divmod(d, DUOS_PER_BATCH)
             last = d + 1 == DUOS
             if part == 0:
                 open_batch(b)
-            if not last:
-                transpose_duo(d + 1)
+            if d + AHEAD < DUOS:
+                transpose_duo(d + AHEAD)
             project_duo(d)
-            if not last:
-                quantise_duo(d + 1)
             rotate_duo(d, nc.vector if last else nc.gpsimd)
+            if d + AHEAD < DUOS:
+                quantise_duo(d + AHEAD)
             copy_v(d)
             quad, rest = divmod(d + 1, DUOS_PER_QUAD)
             if rest == 0 and quad - 1 + LOADS_AHEAD < QUADS:

@@ -31,7 +31,7 @@ DUOS_PER_QUAD = QUAD // DUO
 DUOS_PER_BATCH = TILES // DUO
 ROTATED_HEADS = 2 * HEADS
 AHEAD = 2
-LOADS_AHEAD = 12
+LOADS_AHEAD = 8
 
 FLOPS = 2 * BATCH * SEQ * C * 3 * FEATURES
 
@@ -50,27 +50,29 @@ def tile_groupqueryatention_pa_t_kernel(tc, x, angles, wq, wk, wv, out_0, out_1,
 
         x_tiles = {}
 
-        def load_x(n, pieces=1):
+        def load_x(n, a0=0, a1=QUAD):
             b, half = divmod(n, QUADS_PER_BATCH)
-            x_sb = x_pool.tile([P, QUAD, C], BF16)
+            if a0 == 0:
+                x_sb = x_pool.tile([P, QUAD, C], BF16)
+                x_tiles[n] = x_sb
             rows = x[b].rearrange("(p j) c -> p j c", j=TILES)
-            step = QUAD // pieces
-            for i in range(0, QUAD, step):
-                nc.sync.dma_start(
-                    out=x_sb[:, i : i + step, :], in_=rows[:, half * QUAD + i : half * QUAD + i + step, :]
-                )
-            x_tiles[n] = x_sb
+            nc.sync.dma_start(
+                out=x_tiles[n][:, a0:a1, :], in_=rows[:, half * QUAD + a0 : half * QUAD + a1, :]
+            )
 
-        load_x(0, pieces=QUAD)
         angles_bf = const.tile([P, TILES, PAIRS], BF16)
-        nc.scalar.dma_start(out=angles_bf[:], in_=angles.rearrange("(p j) i -> p j i", j=TILES))
+        nc.sync.dma_start(out=angles_bf[:], in_=angles.rearrange("(p j) i -> p j i", j=TILES))
+        load_x(0, 0, DUO)
         w_raw = const.tile([P, 3, PASSES, PACK, FEATURES], BF16)
         for m, w in enumerate((wq, wk, wv)):
-            nc.scalar.dma_start(
+            nc.sync.dma_start(
                 out=w_raw[:, m].rearrange("p g t n -> p g (t n)"),
                 in_=w.rearrange("(g p t) n -> p g (t n)", g=PASSES, t=PACK),
             )
-        for n in range(1, LOADS_AHEAD):
+        load_x(0, DUO, QUAD)
+        load_x(1, 0, DUO)
+        load_x(1, DUO, QUAD)
+        for n in range(2, LOADS_AHEAD):
             load_x(n)
 
         identity = const.tile([P, P], F32)
@@ -149,13 +151,19 @@ def tile_groupqueryatention_pa_t_kernel(tc, x, angles, wq, wk, wv, out_0, out_1,
 
         def project_duo(d):
             codes, scales = x_operands[d]
-            qk_ps = psum_qk.tile([P, DUO, 2 * FEATURES], F32)
             v_ps = psum_v.tile([P, DUO, FEATURES], F32)
+            qk_banks = []
             for a in range(DUO):
-                for acc, w_codes, w_scales in ((qk_ps, wqk_codes, wqk_scales), (v_ps, wv_codes, wv_scales)):
+                if a == 0 or d + 1 == DUOS:
+                    qk_ps = psum_qk.tile([P, DUO, 2 * FEATURES], F32)
+                qk_banks.append(qk_ps)
+                for acc, w_codes, w_scales in (
+                    (qk_ps[:, a, :], wqk_codes, wqk_scales),
+                    (v_ps[:, a, :], wv_codes, wv_scales),
+                ):
                     for g in range(PASSES):
                         nc.tensor.matmul_mx(
-                            out=acc[:, a, :],
+                            out=acc,
                             lhsT=codes[:, a, g, :].bitcast(FP8X4),
                             lhsT_scale=scales[:, a, g, :],
                             rhs=w_codes[:, g, :].bitcast(FP8X4),
@@ -163,21 +171,21 @@ def tile_groupqueryatention_pa_t_kernel(tc, x, angles, wq, wk, wv, out_0, out_1,
                             start=(g == 0),
                             stop=(g == PASSES - 1),
                         )
-            sums[d] = (qk_ps, v_ps)
+            sums[d] = (qk_banks, v_ps)
 
         def open_batch(b):
             rotated = results.tile([P, ROTATED_HEADS, TILES, HEAD_DIM], F32)
             v_sb = results.tile([P, HEADS, TILES, HEAD_DIM], F32)
             batch_tiles[b] = (rotated, v_sb)
 
-        def rotate_duo(d, adder):
+        def rotate(d, a0, a1, adder):
             b, part = divmod(d, DUOS_PER_BATCH)
             rotated = batch_tiles[b][0]
-            qk_ps = sums[d][0]
-            js = slice(part * DUO, (part + 1) * DUO)
-            odd_part = results.tile([P, ROTATED_HEADS, DUO, HEAD_DIM], F32)
-            shape = [P, DUO, ROTATED_HEADS, PAIRS, 2]
-            pairs = qk_ps[:].rearrange("p a (q i two) -> p a q i two", q=ROTATED_HEADS, two=2)
+            qk_ps = sums[d][0][a0]
+            js = slice(part * DUO + a0, part * DUO + a1)
+            odd_part = results.tile([P, ROTATED_HEADS, a1 - a0, HEAD_DIM], F32)
+            shape = [P, a1 - a0, ROTATED_HEADS, PAIRS, 2]
+            pairs = qk_ps[:, a0:a1, :].rearrange("p a (q i two) -> p a q i two", q=ROTATED_HEADS, two=2)
             nc.vector.tensor_tensor(
                 out=rotated[:, :, js, :].rearrange("p q a (i two) -> p a q i two", two=2),
                 in0=pairs[:, :, :, :, 0:1].to_broadcast(shape),
@@ -220,7 +228,11 @@ def tile_groupqueryatention_pa_t_kernel(tc, x, angles, wq, wk, wv, out_0, out_1,
             if d + AHEAD < DUOS:
                 transpose_duo(d + AHEAD)
             project_duo(d)
-            rotate_duo(d, nc.vector if last else nc.gpsimd)
+            if last:
+                rotate(d, 0, 1, nc.gpsimd)
+                rotate(d, 1, DUO, nc.vector)
+            else:
+                rotate(d, 0, DUO, nc.gpsimd)
             if d + AHEAD < DUOS:
                 quantise_duo(d + AHEAD)
             copy_v(d)

import math
from contextlib import ExitStack

import concourse.mybir as mybir
from concourse.masks import make_identity

F32 = mybir.dt.float32
BF16 = mybir.dt.bfloat16
U32 = mybir.dt.uint32
U8 = mybir.dt.uint8
FP8X4 = mybir.dt.float8_e4m3fn_x4
ALU = mybir.AluOpType
ACT = mybir.ActivationFunctionType

P = 128
BATCH, SEQ, C = 8, 1024, 1024
HEADS, HEAD_DIM = 2, 64
FEATURES = HEADS * HEAD_DIM
PAIRS = HEAD_DIM // 2
PACK = 4
K_PASS = P * PACK
PASSES = C // K_PASS
WORDS = C // 2
TILES = SEQ // P
QUAD = 4
DUO = 2
QUADS = BATCH * TILES // QUAD
QUADS_PER_BATCH = TILES // QUAD
DUOS = BATCH * TILES // DUO
DUOS_PER_QUAD = QUAD // DUO
DUOS_PER_BATCH = TILES // DUO
ROTATED_HEADS = 2 * HEADS
AHEAD = 2
LOADS_AHEAD = 8

FLOPS = 2 * BATCH * SEQ * C * 3 * FEATURES


def tile_groupqueryatention_pa_t_kernel(tc, x, angles, wq, wk, wv, out_0, out_1, out_2):
    nc = tc.nc
    with ExitStack() as ctx:
        const = ctx.enter_context(tc.tile_pool(name="const", bufs=1))
        x_pool = ctx.enter_context(tc.tile_pool(name="x", bufs=LOADS_AHEAD))
        stage = ctx.enter_context(tc.tile_pool(name="stage", bufs=AHEAD + 2))
        results = ctx.enter_context(tc.tile_pool(name="results", bufs=3))
        psum_xt = ctx.enter_context(tc.psum_pool(name="psum_xt", bufs=4))
        psum_qk = ctx.enter_context(tc.psum_pool(name="psum_qk", bufs=3))
        psum_v = ctx.enter_context(tc.psum_pool(name="psum_v", bufs=1))
        ctx.enter_context(tc.manual_schedule())

        x_tiles = {}

        def load_x(n, a0=0, a1=QUAD):
            b, half = divmod(n, QUADS_PER_BATCH)
            if a0 == 0:
                x_sb = x_pool.tile([P, QUAD, C], BF16)
                x_tiles[n] = x_sb
            rows = x[b].rearrange("(p j) c -> p j c", j=TILES)
            nc.sync.dma_start(
                out=x_tiles[n][:, a0:a1, :], in_=rows[:, half * QUAD + a0 : half * QUAD + a1, :]
            )

        angles_bf = const.tile([P, TILES, PAIRS], BF16)
        nc.sync.dma_start(out=angles_bf[:], in_=angles.rearrange("(p j) i -> p j i", j=TILES))
        load_x(0, 0, DUO)
        w_raw = const.tile([P, 3, PASSES, PACK, FEATURES], BF16)
        for m, w in enumerate((wq, wk, wv)):
            nc.sync.dma_start(
                out=w_raw[:, m].rearrange("p g t n -> p g (t n)"),
                in_=w.rearrange("(g p t) n -> p g (t n)", g=PASSES, t=PACK),
            )
        load_x(0, DUO, QUAD)
        load_x(1, 0, DUO)
        load_x(1, DUO, QUAD)
        for n in range(2, LOADS_AHEAD):
            load_x(n)

        identity = const.tile([P, P], F32)
        make_identity(nc, identity[:])

        cos_arg = const.tile([P, TILES, PAIRS], F32)
        nc.vector.scalar_tensor_tensor(
            out=cos_arg[:], in0=angles_bf[:], scalar=-1.0, in1=angles_bf[:], op0=ALU.mult, op1=ALU.max
        )
        nc.vector.tensor_scalar(
            out=cos_arg[:], in0=cos_arg[:], scalar1=-1.0, scalar2=math.pi / 2, op0=ALU.mult, op1=ALU.add
        )
        trig = const.tile([P, TILES, 3, PAIRS], F32)
        nc.scalar.activation(out=trig[:, :, 2, :], in_=angles_bf[:], func=ACT.Sin)
        nc.scalar.activation(out=trig[:, :, 0, :], in_=angles_bf[:], func=ACT.Sin, scale=-1.0)
        nc.scalar.activation(out=trig[:, :, 1, :], in_=cos_arg[:], func=ACT.Sin)

        wqk_grouped = const.tile([P, PASSES, 2 * FEATURES, PACK], BF16, align_bytes=64)
        wv_grouped = const.tile([P, PASSES, FEATURES, PACK], BF16, align_bytes=64)
        for g in range(PASSES):
            nc.vector.tensor_copy(
                out=wqk_grouped[:, g].rearrange("p (m n) t -> p m n t", m=2),
                in_=w_raw[:, 0:2, g].rearrange("p m t n -> p m n t"),
            )
        for g in range(PASSES):
            nc.vector.tensor_copy(out=wv_grouped[:, g], in_=w_raw[:, 2, g].rearrange("p t n -> p n t"))
        wqk_codes = const.tile([P, PASSES, 2 * FEATURES], U32, align_bytes=64)
        wqk_scales = const.tile([P, PASSES, 2 * FEATURES], U8, align_bytes=64)
        wv_codes = const.tile([P, PASSES, FEATURES], U32, align_bytes=64)
        wv_scales = const.tile([P, PASSES, FEATURES], U8, align_bytes=64)
        nc.vector.quantize_mx(
            out=wqk_codes[:].rearrange("p g n -> p (g n)").bitcast(FP8X4),
            scales=wqk_scales[:].rearrange("p g n -> p (g n)"),
            in_=wqk_grouped[:].rearrange("p g n t -> p (g n t)"),
        )
        nc.vector.quantize_mx(
            out=wv_codes[:].rearrange("p g n -> p (g n)").bitcast(FP8X4),
            scales=wv_scales[:].rearrange("p g n -> p (g n)"),
            in_=wv_grouped[:].rearrange("p g n t -> p (g n t)"),
        )

        cos_sin = const.tile([P, TILES, PAIRS, 2], F32)
        negsin_cos = const.tile([P, TILES, PAIRS, 2], F32)

        def interleave_tables():
            nc.vector.tensor_copy(out=cos_sin[:], in_=trig[:, :, 1:3].rearrange("p j two i -> p j i two"))
            nc.vector.tensor_copy(out=negsin_cos[:], in_=trig[:, :, 0:2].rearrange("p j two i -> p j i two"))

        grouped_tiles = {}
        x_operands = {}
        sums = {}
        batch_tiles = {}

        def transpose_duo(d):
            x_words = x_tiles[d // DUOS_PER_QUAD][:].bitcast(F32)
            grouped = stage.tile([P, DUO, PASSES, P, 2], F32, align_bytes=64)
            for a in range(DUO):
                j = (d % DUOS_PER_QUAD) * DUO + a
                xt = psum_xt.tile([P, WORDS // P, P], F32)
                for c in range(WORDS // P):
                    g, u = divmod(c, 2)
                    words = x_words[:, j, g * 2 * P + u : (g + 1) * 2 * P : 2]
                    nc.tensor.transpose(xt[:, c, :], words, identity[:])
                nc.scalar.copy(out=grouped[:, a], in_=xt[:].rearrange("p (g u) r -> p g r u", u=2))
            grouped_tiles[d] = grouped

        def quantise_duo(d):
            codes = stage.tile([P, DUO, PASSES, P], U32, align_bytes=64)
            scales = stage.tile([P, DUO, PASSES, P], U8, align_bytes=64)
            nc.vector.quantize_mx(
                out=codes[:].rearrange("p a g r -> p (a g r)").bitcast(FP8X4),
                scales=scales[:].rearrange("p a g r -> p (a g r)"),
                in_=grouped_tiles[d][:].rearrange("p a g r u -> p (a g r u)").bitcast(BF16),
            )
            x_operands[d] = (codes, scales)

        def project_duo(d):
            codes, scales = x_operands[d]
            v_ps = psum_v.tile([P, DUO, FEATURES], F32)
            qk_banks = []
            for a in range(DUO):
                if a == 0 or d + 1 == DUOS:
                    qk_ps = psum_qk.tile([P, DUO, 2 * FEATURES], F32)
                qk_banks.append(qk_ps)
                for acc, w_codes, w_scales in (
                    (qk_ps[:, a, :], wqk_codes, wqk_scales),
                    (v_ps[:, a, :], wv_codes, wv_scales),
                ):
                    for g in range(PASSES):
                        nc.tensor.matmul_mx(
                            out=acc,
                            lhsT=codes[:, a, g, :].bitcast(FP8X4),
                            lhsT_scale=scales[:, a, g, :],
                            rhs=w_codes[:, g, :].bitcast(FP8X4),
                            rhs_scale=w_scales[:, g, :],
                            start=(g == 0),
                            stop=(g == PASSES - 1),
                        )
            sums[d] = (qk_banks, v_ps)

        def open_batch(b):
            rotated = results.tile([P, ROTATED_HEADS, TILES, HEAD_DIM], F32)
            v_sb = results.tile([P, HEADS, TILES, HEAD_DIM], F32)
            batch_tiles[b] = (rotated, v_sb)

        def rotate(d, a0, a1, adder):
            b, part = divmod(d, DUOS_PER_BATCH)
            rotated = batch_tiles[b][0]
            qk_ps = sums[d][0][a0]
            js = slice(part * DUO + a0, part * DUO + a1)
            odd_part = results.tile([P, ROTATED_HEADS, a1 - a0, HEAD_DIM], F32)
            shape = [P, a1 - a0, ROTATED_HEADS, PAIRS, 2]
            pairs = qk_ps[:, a0:a1, :].rearrange("p a (q i two) -> p a q i two", q=ROTATED_HEADS, two=2)
            nc.vector.tensor_tensor(
                out=rotated[:, :, js, :].rearrange("p q a (i two) -> p a q i two", two=2),
                in0=pairs[:, :, :, :, 0:1].to_broadcast(shape),
                in1=cos_sin[:, js].unsqueeze(2).to_broadcast(shape),
                op=ALU.mult,
            )
            nc.vector.tensor_tensor(
                out=odd_part[:].rearrange("p q a (i two) -> p a q i two", two=2),
                in0=pairs[:, :, :, :, 1:2].to_broadcast(shape),
                in1=negsin_cos[:, js].unsqueeze(2).to_broadcast(shape),
                op=ALU.mult,
            )
            adder.tensor_tensor(out=rotated[:, :, js, :], in0=rotated[:, :, js, :], in1=odd_part[:], op=ALU.add)

        def copy_v(d):
            b, part = divmod(d, DUOS_PER_BATCH)
            js = slice(part * DUO, (part + 1) * DUO)
            nc.scalar.copy(
                out=batch_tiles[b][1][:, :, js, :].rearrange("p h a d -> p a h d"),
                in_=sums[d][1][:].rearrange("p a (h d) -> p a h d", h=HEADS),
            )

        def store(b, j0, j1):
            rotated, v_sb = batch_tiles[b]
            for dram, heads in ((out_2, v_sb[:]), (out_0, rotated[:, 0:HEADS]), (out_1, rotated[:, HEADS:])):
                nc.sync.dma_start(
                    out=dram[b].rearrange("h (p j) d -> p h j d", j=TILES)[:, :, j0:j1, :],
                    in_=heads[:, :, j0:j1, :],
                )

        for d in range(AHEAD):
            transpose_duo(d)
            quantise_duo(d)
        interleave_tables()
        for d in range(DUOS):
            b, part = divmod(d, DUOS_PER_BATCH)
            last = d + 1 == DUOS
            if part == 0:
                open_batch(b)
            if d + AHEAD < DUOS:
                transpose_duo(d + AHEAD)
            project_duo(d)
            if last:
                rotate(d, 0, 1, nc.gpsimd)
                rotate(d, 1, DUO, nc.vector)
            else:
                rotate(d, 0, DUO, nc.gpsimd)
            if d + AHEAD < DUOS:
                quantise_duo(d + AHEAD)
            copy_v(d)
            quad, rest = divmod(d + 1, DUOS_PER_QUAD)
            if rest == 0 and quad - 1 + LOADS_AHEAD < QUADS:
                load_x(quad - 1 + LOADS_AHEAD)
            if b + 1 < BATCH:
                if part + 1 == DUOS_PER_BATCH:
                    store(b, 0, TILES)
            else:
                store(b, part * DUO, (part + 1) * DUO)
